import numpy as np
import ml_dtypes


def mxq(x, axis, fmt="e4m3"):
    dtype, down = {"e4m3": (ml_dtypes.float8_e4m3fn, 7), "e5m2": (ml_dtypes.float8_e5m2, 14)}[fmt]
    v = np.moveaxis(np.asarray(x, np.float32).astype(ml_dtypes.bfloat16).astype(np.float64), axis, -1)
    blocks = v.reshape(v.shape[:-1] + (-1, 32))
    amax = np.abs(blocks).max(-1, keepdims=True)
    byte = np.maximum(np.where(amax > 0, np.frexp(amax)[1] - 1 + 127, 0) - down, 1)
    scale = np.exp2(byte - 127.0)
    codes = (blocks / scale).astype(np.float32).astype(dtype).astype(np.float64)
    return np.moveaxis((codes * scale).reshape(v.shape), -1, axis)


WIDE = False


def mx_kscale(k):
    if not WIDE:
        return np.ones(k)
    levels = np.array([10, -10, 5, -5, 0])
    if k % 512:
        return np.exp2(np.random.permutation(np.resize(levels, k // 32))).repeat(32)
    a = np.empty((k // 512, 16))
    for p in range(k // 512):
        a[p, :8] = np.random.permutation(np.resize(levels, 8))
        for g in range(8):
            far = levels[np.abs(levels - a[p, g]) >= 10]
            a[p, g + 8] = far[np.random.randint(len(far))]
    return np.exp2(a.ravel()).repeat(32)


BF16 = ml_dtypes.bfloat16


def bf(x):
    return np.asarray(x, np.float32).astype(BF16)


def f64(x):
    return np.asarray(x).astype(np.float64)


B, N, HH, WW, TC, IC, DQK = 3, 256, 32, 32, 1024, 1024, 512
M = HH * WW
AQK = np.sqrt(2.0) / DQK ** 0.25


def draw0():
    s = mx_kscale(TC)
    t = mx_kscale(DQK)
    return {"x1": bf(np.random.standard_normal((B, N, TC)) * s),
            "Wq": bf(np.random.standard_normal((TC, DQK)) * AQK / np.sqrt(TC) / s[:, None] * t),
            "bq": bf(np.random.standard_normal(DQK) * 0.25 * AQK * t),
            "k_img": bf(np.random.standard_normal((B, M, DQK)) * AQK / t),
            "masks": bf(np.random.uniform(size=(B, N, M)) > 0.2)}


def core(x1, Wq, bq, k_img, masks):
    q = (mxq(f64(x1), 2, "e4m3") @ mxq(f64(Wq), 0, "e4m3")) + f64(bq)
    s = mxq(q, 2, "e4m3") @ mxq(f64(k_img), 2, "e4m3").transpose(0, 2, 1)
    e = np.exp(s - s.max(-1, keepdims=True))
    return e / e.sum(-1, keepdims=True) * f64(masks)


def e4m3fn_bytes(y):
    return np.clip(np.asarray(y, np.float64), -448.0, 448.0).astype(np.float32).astype(ml_dtypes.float8_e4m3fn).view(np.uint8)


def e4m3fn_values(b):
    return np.asarray(b, np.uint8).view(ml_dtypes.float8_e4m3fn).astype(np.float64)


def setup_inputs():
    d = draw0()
    x0 = np.asarray(d['k_img']).astype(np.float64)
    s = (np.max(np.abs(x0), axis=(0, 1), keepdims=True) / 448.0).astype(np.float32)
    out = {}
    for k, v in d.items():
        if k == 'k_img':
            out['k_img_bytes'] = e4m3fn_bytes(x0 / s.astype(np.float64))
            out['k_img_scale'] = s
        else:
            out[k] = v
    return out


def reference(x1, Wq, bq, k_img_bytes, k_img_scale, masks):
    return core(x1, Wq, bq, e4m3fn_values(k_img_bytes) * k_img_scale.astype(np.float64), masks)

@@ -1,0 +1,357 @@
+from contextlib import ExitStack
+
+import concourse.mybir as mybir
+from concourse.masks import make_identity
+
+B, N, M, TC, DQK = 3, 256, 1024, 1024, 512
+FLOPS = 2 * B * N * TC * DQK + 2 * B * N * DQK * M
+
+F32 = mybir.dt.float32
+BF16 = mybir.dt.bfloat16
+U32 = mybir.dt.uint32
+U8 = mybir.dt.uint8
+FP8 = mybir.dt.float8_e4m3fn
+FP8X4 = mybir.dt.float8_e4m3fn_x4
+ALU = mybir.AluOpType
+ACT = mybir.ActivationFunctionType
+
+P = 128
+HALF = 512
+
+
+def tile_text2imgca_pa_kernel(tc, x1, Wq, bq, k_img_bytes, k_img_scale, masks, out):
+    nc = tc.nc
+    with ExitStack() as ctx:
+        keep = ctx.enter_context(tc.tile_pool(name="keep", bufs=1))
+        ring = ctx.enter_context(tc.tile_pool(name="ring", bufs=3))
+        psum = ctx.enter_context(tc.psum_pool(name="psum", bufs=1))
+        ctx.enter_context(tc.manual_schedule())
+
+        def sb(name, shape, dtype):
+            return keep.tile(shape, dtype, name=name, align_bytes=64)
+
+        def quantize(name, src, words):
+            codes = sb(name + "_codes", [P, words], U32)
+            scales = sb(name + "_scales", [P, words], U8)
+            nc.vector.quantize_mx(out=codes[:].bitcast(FP8X4), scales=scales[:], in_=src)
+            return codes, scales
+
+        ident = sb("ident", [P, P], F32)
+        make_identity(nc, ident[:])
+
+        key_bytes, x_rows, w_rows, mask_rows = {}, {}, {}, {}
+
+        def load_keys(b, h):
+            t = sb("key_bytes_%d_%d" % (b, h), [P, 4 * DQK], U8)
+            src = k_img_bytes[b, h * HALF : (h + 1) * HALF, :]
+            nc.sync.dma_start(out=t[:], in_=src.rearrange("(p a) d -> p (a d)", a=4))
+            key_bytes[b, h] = t
+
+        def load_x(b, a):
+            t = sb("x_rows_%d_%d" % (b, a), [P, TC], BF16)
+            nc.sync.dma_start(out=t[:], in_=x1[b, a * P : (a + 1) * P, :])
+            x_rows[b, a] = t
+
+        def load_w(g):
+            t = sb("w_rows_%d" % g, [P, 4 * DQK], BF16)
+            src = Wq[g * HALF : (g + 1) * HALF, :]
+            nc.sync.dma_start(out=t[:], in_=src.rearrange("(p j) d -> p (j d)", j=4))
+            w_rows[g] = t
+
+        def load_mask(b):
+            t = sb("mask_rows_%d" % b, [P, 2, M], BF16)
+            nc.sync.dma_start(out=t[:], in_=masks[b].rearrange("(a p) m -> p a m", p=P))
+            mask_rows[b] = t
+
+        scale_cols = sb("scale_cols", [P, 4], F32)
+        nc.sync.dma_start(out=scale_cols[:], in_=k_img_scale.rearrange("o i (p c) -> p (o i c)", c=4))
+        load_keys(0, 0)
+        load_w(0)
+        load_keys(0, 1)
+        load_w(1)
+        load_x(0, 0)
+        load_x(0, 1)
+        bias = sb("bias", [P, 4], BF16)
+        nc.sync.dma_start(out=bias[:], in_=bq.rearrange("(p t) -> p t", t=4))
+        load_keys(1, 0)
+        load_keys(1, 1)
+        load_x(1, 0)
+        load_x(1, 1)
+        load_mask(0)
+        load_keys(2, 0)
+        load_keys(2, 1)
+        load_x(2, 0)
+        load_x(2, 1)
+        load_mask(1)
+        load_mask(2)
+
+        scale_bank = psum.tile([P, DQK], F32, name="scale_bank")
+        for c in range(4):
+            nc.tensor.transpose(scale_bank[:, c::4], scale_cols[:, c : c + 1].to_broadcast([P, P]), ident[:])
+
+        key_wide, key_bank, key_in, key_mx = {}, {}, {}, {}
+
+        def key_scale(b, h, s):
+            t = sb("key_wide_%d_%d_%d" % (b, h, s), [P, 2, DQK], BF16)
+            for a in range(2):
+                row = 2 * s + a
+                codes = key_bytes[b, h][:, row * DQK : (row + 1) * DQK].bitcast(FP8)
+                nc.vector.tensor_tensor(out=t[:, a, :], in0=codes, in1=scale_bank[:], op=ALU.mult)
+            key_wide[b, h, s] = t
+
+        def key_turn(b, h, s):
+            bank = psum.tile([P, 4, P], F32, name="key_bank", tag="turn", bufs=3)
+            for a in range(2):
+                words = key_wide[b, h, s][:, a, :].bitcast(F32)
+                for u in range(2):
+                    nc.tensor.transpose(bank[:, 2 * a + u, :], words[:, u::2], ident[:])
+            key_bank[b, h, s] = bank
+
+        def key_copy(b, h, s):
+            if s == 0:
+                key_in[b, h] = sb("key_in_%d_%d" % (b, h), [P, P, 2, 4], F32)
+            nc.scalar.copy(out=key_in[b, h][:, :, s, :], in_=key_bank[b, h, s][:].rearrange("p j n -> p n j"))
+
+        def key_quantize(b, h):
+            src = key_in[b, h][:].rearrange("p n s j -> p (n s j)").bitcast(BF16)
+            key_mx[b, h] = quantize("key_%d_%d" % (b, h), src, HALF)
+
+        w_in, w_mx = {}, {}
+
+        def w_interleave(g, u):
+            if u == 0:
+                w_in[g] = sb("w_in_%d" % g, [P, 4, P, 4], BF16)
+            src = w_rows[g][:].rearrange("p (j m t) -> p m t j", j=4, t=4)
+            dst = w_in[g][:].rearrange("p t m j -> p m t j")
+            nc.scalar.copy(out=dst[:, u * 64 : (u + 1) * 64], in_=src[:, u * 64 : (u + 1) * 64])
+
+        def w_quantize(g):
+            w_mx[g] = quantize("w_%d" % g, w_in[g][:].rearrange("p t m j -> p (t m j)"), DQK)
+
+        x_bank, x_in, x_mx = {}, {}, {}
+
+        def x_turn(b, a):
+            bank = psum.tile([P, 4, P], F32, name="x_bank", tag="turn", bufs=3)
+            words = x_rows[b, a][:].bitcast(F32)
+            for g in range(2):
+                for u in range(2):
+                    nc.tensor.transpose(bank[:, 2 * g + u, :], words[:, 256 * g + u : 256 * (g + 1) : 2], ident[:])
+            x_bank[b, a] = bank
+
+        def x_copy(b, a):
+            if a == 0:
+                x_in[b] = sb("x_in_%d" % b, [P, 2, N, 2], F32)
+            nc.scalar.copy(
+                out=x_in[b][:, :, a * P : (a + 1) * P, :],
+                in_=x_bank[b, a][:].rearrange("p (g u) n -> p g n u", u=2),
+            )
+
+        def x_quantize(b):
+            x_mx[b] = quantize("x_%d" % b, x_in[b][:].rearrange("p g n u -> p (g n u)").bitcast(BF16), 2 * N)
+
+        q_bank, q_planes, q_in, q_mx = {}, {}, {}, {}
+
+        def q_matmul(b):
+            x_codes, x_scales = x_mx[b]
+            for u in range(2):
+                bank = psum.tile([P, 2, N], F32, name="q_bank", tag="sums", bufs=4)
+                for e in range(2):
+                    cols = slice((2 * u + e) * P, (2 * u + e + 1) * P)
+                    for g in range(2):
+                        w_codes, w_scales = w_mx[g]
+                        nc.tensor.matmul_mx(
+                            out=bank[:, e, :],
+                            lhsT=w_codes[:, cols].bitcast(FP8X4),
+                            lhsT_scale=w_scales[:, cols],
+                            rhs=x_codes[:, g * N : (g + 1) * N].bitcast(FP8X4),
+                            rhs_scale=x_scales[:, g * N : (g + 1) * N],
+                            start=(g == 0),
+                            stop=(g == 1),
+                        )
+                q_bank[b, u] = bank
+
+        def q_bias(b):
+            q_planes[b] = sb("q_planes_%d" % b, [P, 4, N], BF16)
+            for t in range(4):
+                nc.scalar.activation(
+                    out=q_planes[b][:, t, :], in_=q_bank[b, t // 2][:, t % 2, :], func=ACT.Identity, bias=bias[:, t : t + 1]
+                )
+
+        def q_interleave(b):
+            q_in[b] = sb("q_in_%d" % b, [P, N, 4], BF16)
+            nc.vector.tensor_copy(out=q_in[b][:], in_=q_planes[b][:].rearrange("p t n -> p n t"))
+
+        def q_quantize(b):
+            q_mx[b] = quantize("q_%d" % b, q_in[b][:].rearrange("p n t -> p (n t)"), N)
+
+        score_bank, neg, low, expd, total, inv = {}, {}, {}, {}, {}, {}
+
+        def scores(i, h):
+            b, a = divmod(i, 2)
+            q_codes, q_scales = q_mx[b]
+            k_codes, k_scales = key_mx[b, h]
+            bank = psum.tile([P, HALF], F32, name="score_bank", tag="sums", bufs=4)
+            nc.tensor.matmul_mx(
+                out=bank[:],
+                lhsT=q_codes[:, a * P : (a + 1) * P].bitcast(FP8X4),
+                lhsT_scale=q_scales[:, a * P : (a + 1) * P],
+                rhs=k_codes[:].bitcast(FP8X4),
+                rhs_scale=k_scales[:],
+                start=True,
+                stop=True,
+            )
+            score_bank[i, h] = bank
+
+        def negate_and_min(i, h):
+            if h == 0:
+                neg[i] = ring.tile([P, M], F32, name="neg_scores")
+            low[i, h] = sb("low_%d_%d" % (i, h), [P, 1], F32)
+            nc.vector.tensor_scalar(
+                out=neg[i][:, h * HALF : (h + 1) * HALF],
+                in0=score_bank[i, h][:],
+                scalar1=-1.0,
+                scalar2=low[i, 0][:] if h else None,
+                op0=ALU.mult,
+                op1=ALU.min,
+                accum_out=low[i, h][:],
+            )
+
+        def exponentials(i):
+            expd[i] = ring.tile([P, M], F32, name="expd")
+            total[i] = sb("total_%d" % i, [P, 1], F32)
+            nc.scalar.activation(
+                out=expd[i][:], in_=neg[i][:], func=ACT.Exp, scale=-1.0, bias=low[i, 1][:], accum_out=total[i][:]
+            )
+
+        def invert(i):
+            inv[i] = sb("inv_%d" % i, [P, 1], F32)
+            nc.vector.reciprocal(out=inv[i][:], in_=total[i][:])
+
+        def finish(i, parts=1):
+            b, a = divmod(i, 2)
+            width = M // parts
+            for part in range(parts):
+                cols = slice(part * width, (part + 1) * width)
+                res = sb("res_%d_%d" % (i, part), [P, width], F32)
+                nc.vector.scalar_tensor_tensor(
+                    out=res[:], in0=expd[i][:, cols], scalar=inv[i][:], in1=mask_rows[b][:, a, cols], op0=ALU.mult, op1=ALU.mult
+                )
+                nc.sync.dma_start(out=out[b, a * P : (a + 1) * P, cols], in_=res[:])
+
+        key_scale(0, 0, 0)
+        key_scale(0, 0, 1)
+        key_scale(0, 1, 0)
+        key_scale(0, 1, 1)
+        w_interleave(0, 0)
+        w_interleave(0, 1)
+        w_interleave(1, 0)
+        w_interleave(1, 1)
+        x_turn(0, 0)
+        x_turn(0, 1)
+        key_turn(0, 0, 0)
+        w_quantize(0)
+        key_scale(1, 0, 0)
+        key_scale(1, 0, 1)
+        w_quantize(1)
+        x_copy(0, 0)
+        x_copy(0, 1)
+        key_copy(0, 0, 0)
+        key_turn(0, 0, 1)
+        x_quantize(0)
+        key_scale(1, 1, 0)
+        key_scale(1, 1, 1)
+        key_copy(0, 0, 1)
+        q_matmul(0)
+        key_turn(0, 1, 0)
+        key_turn(0, 1, 1)
+        x_turn(1, 0)
+        key_quantize(0, 0)
+        key_scale(2, 0, 0)
+        key_scale(2, 0, 1)
+        q_bias(0)
+        key_copy(0, 1, 0)
+        key_copy(0, 1, 1)
+        x_copy(1, 0)
+        x_turn(1, 1)
+        key_turn(1, 0, 0)
+        key_turn(1, 0, 1)
+        q_interleave(0)
+        key_quantize(0, 1)
+        q_quantize(0)
+        key_scale(2, 1, 0)
+        x_copy(1, 1)
+        key_copy(1, 0, 0)
+        key_copy(1, 0, 1)
+        scores(0, 0)
+        scores(0, 1)
+        x_quantize(1)
+        key_scale(2, 1, 1)
+        negate_and_min(0, 0)
+        key_quantize(1, 0)
+        negate_and_min(0, 1)
+        q_matmul(1)
+        key_turn(1, 1, 0)
+        key_turn(1, 1, 1)
+        scores(1, 0)
+        scores(1, 1)
+        x_turn(2, 0)
+        q_bias(1)
+        key_copy(1, 1, 0)
+        key_copy(1, 1, 1)
+        exponentials(0)
+        x_copy(2, 0)
+        x_turn(2, 1)
+        key_turn(2, 0, 0)
+        key_turn(2, 0, 1)
+        q_interleave(1)
+        negate_and_min(1, 0)
+        q_quantize(1)
+        negate_and_min(1, 1)
+        key_quantize(1, 1)
+        invert(0)
+        finish(0)
+        x_copy(2, 1)
+        exponentials(1)
+        key_copy(2, 0, 0)
+        key_copy(2, 0, 1)
+        scores(2, 0)
+        scores(2, 1)
+        x_quantize(2)
+        invert(1)
+        negate_and_min(2, 0)
+        finish(1)
+        negate_and_min(2, 1)
+        key_quantize(2, 0)
+        q_matmul(2)
+        scores(3, 0)
+        key_turn(2, 1, 0)
+        key_turn(2, 1, 1)
+        scores(3, 1)
+        negate_and_min(3, 0)
+        q_bias(2)
+        key_copy(2, 1, 0)
+        key_copy(2, 1, 1)
+        exponentials(2)
+        q_interleave(2)
+        negate_and_min(3, 1)
+        q_quantize(2)
+        invert(2)
+        key_quantize(2, 1)
+        finish(2)
+        exponentials(3)
+        scores(4, 0)
+        scores(5, 0)
+        negate_and_min(4, 0)
+        negate_and_min(5, 0)
+        scores(4, 1)
+        scores(5, 1)
+        negate_and_min(4, 1)
+        invert(3)
+        negate_and_min(5, 1)
+        finish(3)
+        exponentials(4)
+        exponentials(5)
+        invert(4)
+        finish(4)
+        invert(5)
+        finish(5, 2)

@@ -16,23 +16,30 @@ ALU = mybir.AluOpType
 ACT = mybir.ActivationFunctionType
 
 P = 128
-HALF = 512
+PACK = 4
+K_PASS = P * PACK
+HALF = M // 2
+W_SPLIT = DQK // 2
+TURN_BANKS = 3
+SUM_BANKS = 4
+RING = 3
+TILE2_ON_GPSIMD = M // 2
 
 
 def tile_text2imgca_pa_kernel(tc, x1, Wq, bq, k_img_bytes, k_img_scale, masks, out):
     nc = tc.nc
     with ExitStack() as ctx:
         keep = ctx.enter_context(tc.tile_pool(name="keep", bufs=1))
-        ring = ctx.enter_context(tc.tile_pool(name="ring", bufs=3))
+        ring = ctx.enter_context(tc.tile_pool(name="ring", bufs=RING))
         psum = ctx.enter_context(tc.psum_pool(name="psum", bufs=1))
         ctx.enter_context(tc.manual_schedule())
 
         def sb(name, shape, dtype):
             return keep.tile(shape, dtype, name=name, align_bytes=64)
 
-        def quantize(name, src, words):
-            codes = sb(name + "_codes", [P, words], U32)
-            scales = sb(name + "_scales", [P, words], U8)
+        def quantize(name, src, columns):
+            codes = sb(name + "_codes", [P, columns], U32)
+            scales = sb(name + "_scales", [P, columns], U8)
             nc.vector.quantize_mx(out=codes[:].bitcast(FP8X4), scales=scales[:], in_=src)
             return codes, scales
 
@@ -42,121 +49,121 @@ def tile_text2imgca_pa_kernel(tc, x1, Wq, bq, k_img_bytes, k_img_scale, masks, o
         key_bytes, x_rows, w_rows, mask_rows = {}, {}, {}, {}
 
         def load_keys(b, h):
-            t = sb("key_bytes_%d_%d" % (b, h), [P, 4 * DQK], U8)
+            tile = sb("key_bytes_%d_%d" % (b, h), [P, PACK * DQK], U8)
             src = k_img_bytes[b, h * HALF : (h + 1) * HALF, :]
-            nc.sync.dma_start(out=t[:], in_=src.rearrange("(p a) d -> p (a d)", a=4))
-            key_bytes[b, h] = t
+            nc.sync.dma_start(out=tile[:], in_=src.rearrange("(p r) d -> p (r d)", r=PACK))
+            key_bytes[b, h] = tile
 
         def load_x(b, a):
-            t = sb("x_rows_%d_%d" % (b, a), [P, TC], BF16)
-            nc.sync.dma_start(out=t[:], in_=x1[b, a * P : (a + 1) * P, :])
-            x_rows[b, a] = t
+            tile = sb("x_rows_%d_%d" % (b, a), [P, TC], BF16)
+            nc.sync.dma_start(out=tile[:], in_=x1[b, a * P : (a + 1) * P, :])
+            x_rows[b, a] = tile
 
-        def load_w(g):
-            t = sb("w_rows_%d" % g, [P, 4 * DQK], BF16)
-            src = Wq[g * HALF : (g + 1) * HALF, :]
-            nc.sync.dma_start(out=t[:], in_=src.rearrange("(p j) d -> p (j d)", j=4))
-            w_rows[g] = t
+        def load_w(g, first, width):
+            tile = sb("w_rows_%d_%d" % (g, first), [P, PACK, width], BF16)
+            src = Wq[g * K_PASS : (g + 1) * K_PASS, first : first + width]
+            nc.sync.dma_start(out=tile[:], in_=src.rearrange("(p j) d -> p j d", j=PACK))
+            w_rows[g, first] = tile
 
         def load_mask(b):
-            t = sb("mask_rows_%d" % b, [P, 2, M], BF16)
-            nc.sync.dma_start(out=t[:], in_=masks[b].rearrange("(a p) m -> p a m", p=P))
-            mask_rows[b] = t
+            tile = sb("mask_rows_%d" % b, [P, 2, M], BF16)
+            nc.sync.dma_start(out=tile[:], in_=masks[b].rearrange("(a p) m -> p a m", p=P))
+            mask_rows[b] = tile
 
-        scale_cols = sb("scale_cols", [P, 4], F32)
-        nc.sync.dma_start(out=scale_cols[:], in_=k_img_scale.rearrange("o i (p c) -> p (o i c)", c=4))
+        scale_cols = sb("scale_cols", [P, PACK], F32)
+        nc.sync.dma_start(out=scale_cols[:], in_=k_img_scale.rearrange("o i (p c) -> p (o i c)", c=PACK))
+        load_w(0, 0, W_SPLIT)
         load_keys(0, 0)
-        load_w(0)
+        load_w(1, 0, DQK)
+        load_w(0, W_SPLIT, W_SPLIT)
         load_keys(0, 1)
-        load_w(1)
         load_x(0, 0)
         load_x(0, 1)
-        bias = sb("bias", [P, 4], BF16)
-        nc.sync.dma_start(out=bias[:], in_=bq.rearrange("(p t) -> p t", t=4))
+        bias = sb("bias", [P, PACK], BF16)
+        nc.sync.dma_start(out=bias[:], in_=bq.rearrange("(p t) -> p t", t=PACK))
         load_keys(1, 0)
-        load_keys(1, 1)
         load_x(1, 0)
         load_x(1, 1)
-        load_mask(0)
-        load_keys(2, 0)
-        load_keys(2, 1)
+        load_keys(1, 1)
         load_x(2, 0)
         load_x(2, 1)
-        load_mask(1)
-        load_mask(2)
+        load_keys(2, 0)
+        load_keys(2, 1)
+        for b in range(B):
+            load_mask(b)
 
         scale_bank = psum.tile([P, DQK], F32, name="scale_bank")
-        for c in range(4):
-            nc.tensor.transpose(scale_bank[:, c::4], scale_cols[:, c : c + 1].to_broadcast([P, P]), ident[:])
+        for c in range(PACK):
+            nc.tensor.transpose(scale_bank[:, c::PACK], scale_cols[:, c : c + 1].to_broadcast([P, P]), ident[:])
 
-        key_wide, key_bank, key_in, key_mx = {}, {}, {}, {}
+        key_wide, key_in, key_mx = {}, {}, {}
 
         def key_scale(b, h, s):
-            t = sb("key_wide_%d_%d_%d" % (b, h, s), [P, 2, DQK], BF16)
-            for a in range(2):
-                row = 2 * s + a
+            tile = sb("key_wide_%d_%d_%d" % (b, h, s), [P, 2, DQK], BF16)
+            for r in range(2):
+                row = 2 * s + r
                 codes = key_bytes[b, h][:, row * DQK : (row + 1) * DQK].bitcast(FP8)
-                nc.vector.tensor_tensor(out=t[:, a, :], in0=codes, in1=scale_bank[:], op=ALU.mult)
-            key_wide[b, h, s] = t
+                nc.vector.tensor_tensor(out=tile[:, r, :], in0=codes, in1=scale_bank[:], op=ALU.mult)
+            key_wide[b, h, s] = tile
 
         def key_turn(b, h, s):
-            bank = psum.tile([P, 4, P], F32, name="key_bank", tag="turn", bufs=3)
-            for a in range(2):
-                words = key_wide[b, h, s][:, a, :].bitcast(F32)
+            bank = psum.tile([P, 4, P], F32, name="key_bank", tag="turn", bufs=TURN_BANKS)
+            for r in range(2):
+                pairs = key_wide[b, h, s][:, r, :].bitcast(F32)
                 for u in range(2):
-                    nc.tensor.transpose(bank[:, 2 * a + u, :], words[:, u::2], ident[:])
-            key_bank[b, h, s] = bank
-
-        def key_copy(b, h, s):
+                    nc.tensor.transpose(bank[:, 2 * r + u, :], pairs[:, u::2], ident[:])
             if s == 0:
                 key_in[b, h] = sb("key_in_%d_%d" % (b, h), [P, P, 2, 4], F32)
-            nc.scalar.copy(out=key_in[b, h][:, :, s, :], in_=key_bank[b, h, s][:].rearrange("p j n -> p n j"))
+            nc.scalar.copy(out=key_in[b, h][:, :, s, :], in_=bank[:].rearrange("p j n -> p n j"))
+
+        def key_scale_and_turn(b, h, s):
+            key_scale(b, h, s)
+            key_turn(b, h, s)
 
         def key_quantize(b, h):
             src = key_in[b, h][:].rearrange("p n s j -> p (n s j)").bitcast(BF16)
             key_mx[b, h] = quantize("key_%d_%d" % (b, h), src, HALF)
 
         w_in, w_mx = {}, {}
+        for g in range(2):
+            w_in[g] = sb("w_in_%d" % g, [P, PACK, P, PACK], BF16)
 
-        def w_interleave(g, u):
-            if u == 0:
-                w_in[g] = sb("w_in_%d" % g, [P, 4, P, 4], BF16)
-            src = w_rows[g][:].rearrange("p (j m t) -> p m t j", j=4, t=4)
+        def w_views(g, first):
+            src = w_rows[g, first][:].rearrange("p j (m t) -> p m t j", t=PACK)
             dst = w_in[g][:].rearrange("p t m j -> p m t j")
-            nc.scalar.copy(out=dst[:, u * 64 : (u + 1) * 64], in_=src[:, u * 64 : (u + 1) * 64])
+            return dst[:, first // PACK : first // PACK + src.shape[1]], src
 
         def w_quantize(g):
             w_mx[g] = quantize("w_%d" % g, w_in[g][:].rearrange("p t m j -> p (t m j)"), DQK)
 
-        x_bank, x_in, x_mx = {}, {}, {}
+        x_in, x_mx = {}, {}
 
         def x_turn(b, a):
-            bank = psum.tile([P, 4, P], F32, name="x_bank", tag="turn", bufs=3)
-            words = x_rows[b, a][:].bitcast(F32)
+            bank = psum.tile([P, 4, P], F32, name="x_bank", tag="turn", bufs=TURN_BANKS)
+            pairs = x_rows[b, a][:].bitcast(F32)
             for g in range(2):
                 for u in range(2):
-                    nc.tensor.transpose(bank[:, 2 * g + u, :], words[:, 256 * g + u : 256 * (g + 1) : 2], ident[:])
-            x_bank[b, a] = bank
-
-        def x_copy(b, a):
+                    first = g * K_PASS // 2
+                    nc.tensor.transpose(bank[:, 2 * g + u, :], pairs[:, first + u : first + K_PASS // 2 : 2], ident[:])
             if a == 0:
                 x_in[b] = sb("x_in_%d" % b, [P, 2, N, 2], F32)
             nc.scalar.copy(
                 out=x_in[b][:, :, a * P : (a + 1) * P, :],
-                in_=x_bank[b, a][:].rearrange("p (g u) n -> p g n u", u=2),
+                in_=bank[:].rearrange("p (g u) n -> p g n u", u=2),
             )
 
         def x_quantize(b):
             x_mx[b] = quantize("x_%d" % b, x_in[b][:].rearrange("p g n u -> p (g n u)").bitcast(BF16), 2 * N)
 
-        q_bank, q_planes, q_in, q_mx = {}, {}, {}, {}
+        q_slices, q_in, q_mx = {}, {}, {}
 
-        def q_matmul(b):
+        def q_project(b):
             x_codes, x_scales = x_mx[b]
-            for u in range(2):
-                bank = psum.tile([P, 2, N], F32, name="q_bank", tag="sums", bufs=4)
+            banks = []
+            for pair in range(2):
+                bank = psum.tile([P, 2, N], F32, name="q_bank", tag="sums", bufs=SUM_BANKS)
                 for e in range(2):
-                    cols = slice((2 * u + e) * P, (2 * u + e + 1) * P)
+                    cols = slice((2 * pair + e) * P, (2 * pair + e + 1) * P)
                     for g in range(2):
                         w_codes, w_scales = w_mx[g]
                         nc.tensor.matmul_mx(
@@ -168,29 +175,27 @@ def tile_text2imgca_pa_kernel(tc, x1, Wq, bq, k_img_bytes, k_img_scale, masks, o
                             start=(g == 0),
                             stop=(g == 1),
                         )
-                q_bank[b, u] = bank
-
-        def q_bias(b):
-            q_planes[b] = sb("q_planes_%d" % b, [P, 4, N], BF16)
-            for t in range(4):
+                banks.append(bank)
+            q_slices[b] = sb("q_slices_%d" % b, [P, PACK, N], BF16)
+            for t in range(PACK):
                 nc.scalar.activation(
-                    out=q_planes[b][:, t, :], in_=q_bank[b, t // 2][:, t % 2, :], func=ACT.Identity, bias=bias[:, t : t + 1]
+                    out=q_slices[b][:, t, :], in_=banks[t // 2][:, t % 2, :], func=ACT.Identity, bias=bias[:, t : t + 1]
                 )
 
-        def q_interleave(b):
-            q_in[b] = sb("q_in_%d" % b, [P, N, 4], BF16)
-            nc.vector.tensor_copy(out=q_in[b][:], in_=q_planes[b][:].rearrange("p t n -> p n t"))
+        def q_interleave(b, copy):
+            q_in[b] = sb("q_in_%d" % b, [P, N, PACK], BF16)
+            copy(out=q_in[b][:], in_=q_slices[b][:].rearrange("p t n -> p n t"))
 
         def q_quantize(b):
             q_mx[b] = quantize("q_%d" % b, q_in[b][:].rearrange("p n t -> p (n t)"), N)
 
-        score_bank, neg, low, expd, total, inv = {}, {}, {}, {}, {}, {}
+        score_bank, negated, low, expd, total, inv, masked = {}, {}, {}, {}, {}, {}, {}
 
         def scores(i, h):
             b, a = divmod(i, 2)
             q_codes, q_scales = q_mx[b]
             k_codes, k_scales = key_mx[b, h]
-            bank = psum.tile([P, HALF], F32, name="score_bank", tag="sums", bufs=4)
+            bank = psum.tile([P, HALF], F32, name="score_bank", tag="sums", bufs=SUM_BANKS)
             nc.tensor.matmul_mx(
                 out=bank[:],
                 lhsT=q_codes[:, a * P : (a + 1) * P].bitcast(FP8X4),
@@ -202,12 +207,12 @@ def tile_text2imgca_pa_kernel(tc, x1, Wq, bq, k_img_bytes, k_img_scale, masks, o
             )
             score_bank[i, h] = bank
 
-        def negate_and_min(i, h):
+        def row_extreme(i, h):
             if h == 0:
-                neg[i] = ring.tile([P, M], F32, name="neg_scores")
+                negated[i] = ring.tile([P, M], F32, name="negated")
             low[i, h] = sb("low_%d_%d" % (i, h), [P, 1], F32)
             nc.vector.tensor_scalar(
-                out=neg[i][:, h * HALF : (h + 1) * HALF],
+                out=negated[i][:, h * HALF : (h + 1) * HALF],
                 in0=score_bank[i, h][:],
                 scalar1=-1.0,
                 scalar2=low[i, 0][:] if h else None,
@@ -220,138 +225,123 @@ def tile_text2imgca_pa_kernel(tc, x1, Wq, bq, k_img_bytes, k_img_scale, masks, o
             expd[i] = ring.tile([P, M], F32, name="expd")
             total[i] = sb("total_%d" % i, [P, 1], F32)
             nc.scalar.activation(
-                out=expd[i][:], in_=neg[i][:], func=ACT.Exp, scale=-1.0, bias=low[i, 1][:], accum_out=total[i][:]
+                out=expd[i][:], in_=negated[i][:], func=ACT.Exp, scale=-1.0, bias=low[i, 1][:], accum_out=total[i][:]
             )
 
         def invert(i):
             inv[i] = sb("inv_%d" % i, [P, 1], F32)
             nc.vector.reciprocal(out=inv[i][:], in_=total[i][:])
 
-        def finish(i, parts=1):
+        def mask_on_gpsimd(i, width):
             b, a = divmod(i, 2)
-            width = M // parts
-            for part in range(parts):
-                cols = slice(part * width, (part + 1) * width)
-                res = sb("res_%d_%d" % (i, part), [P, width], F32)
-                nc.vector.scalar_tensor_tensor(
-                    out=res[:], in0=expd[i][:, cols], scalar=inv[i][:], in1=mask_rows[b][:, a, cols], op0=ALU.mult, op1=ALU.mult
-                )
-                nc.sync.dma_start(out=out[b, a * P : (a + 1) * P, cols], in_=res[:])
+            masked[i] = ring.tile([P, width], F32, name="masked")
+            nc.gpsimd.tensor_tensor(out=masked[i][:], in0=expd[i][:, :width], in1=mask_rows[b][:, a, :width], op=ALU.mult)
 
-        key_scale(0, 0, 0)
-        key_scale(0, 0, 1)
-        key_scale(0, 1, 0)
-        key_scale(0, 1, 1)
-        w_interleave(0, 0)
-        w_interleave(0, 1)
-        w_interleave(1, 0)
-        w_interleave(1, 1)
-        x_turn(0, 0)
-        x_turn(0, 1)
-        key_turn(0, 0, 0)
-        w_quantize(0)
-        key_scale(1, 0, 0)
-        key_scale(1, 0, 1)
-        w_quantize(1)
-        x_copy(0, 0)
-        x_copy(0, 1)
-        key_copy(0, 0, 0)
-        key_turn(0, 0, 1)
+        def normalise_on_scalar(i, width):
+            b, a = divmod(i, 2)
+            res = sb("res_scalar_%d" % i, [P, width], F32)
+            nc.scalar.activation(out=res[:], in_=masked[i][:], func=ACT.Copy, scale=inv[i][:])
+            nc.sync.dma_start(out=out[b, a * P : (a + 1) * P, :width], in_=res[:])
+
+        def finish_on_vector(i, first, width):
+            b, a = divmod(i, 2)
+            cols = slice(first, first + width)
+            res = sb("res_vector_%d_%d" % (i, first), [P, width], F32)
+            nc.vector.scalar_tensor_tensor(
+                out=res[:], in0=expd[i][:, cols], scalar=inv[i][:], in1=mask_rows[b][:, a, cols], op0=ALU.mult, op1=ALU.mult
+            )
+            nc.sync.dma_start(out=out[b, a * P : (a + 1) * P, cols], in_=res[:])
+
+        dst, src = w_views(0, 0)
+        nc.vector.tensor_copy(out=dst, in_=src)
+        dst, src = w_views(1, 0)
+        nc.gpsimd.tensor_scalar(out=dst, in0=src, scalar1=1.0, scalar2=0.0, op0=ALU.mult, op1=ALU.add)
+        dst, src = w_views(0, W_SPLIT)
+        nc.scalar.copy(out=dst, in_=src)
+        for s in range(2):
+            key_scale_and_turn(0, 0, s)
+        for a in range(2):
+            x_turn(0, a)
+        for s in range(2):
+            x_turn(1, s)
+            key_scale_and_turn(0, 1, s)
+        key_scale_and_turn(1, 0, 0)
+
+        for g in range(2):
+            w_quantize(g)
         x_quantize(0)
-        key_scale(1, 1, 0)
-        key_scale(1, 1, 1)
-        key_copy(0, 0, 1)
-        q_matmul(0)
-        key_turn(0, 1, 0)
-        key_turn(0, 1, 1)
-        x_turn(1, 0)
+        q_project(0)
+        key_scale_and_turn(1, 0, 1)
         key_quantize(0, 0)
-        key_scale(2, 0, 0)
-        key_scale(2, 0, 1)
-        q_bias(0)
-        key_copy(0, 1, 0)
-        key_copy(0, 1, 1)
-        x_copy(1, 0)
-        x_turn(1, 1)
-        key_turn(1, 0, 0)
-        key_turn(1, 0, 1)
-        q_interleave(0)
+        for a in range(2):
+            x_turn(2, a)
+        key_scale(1, 1, 0)
+        x_quantize(1)
+        q_project(1)
+        key_turn(1, 1, 0)
+        key_scale(1, 1, 1)
+        q_interleave(0, nc.vector.tensor_copy)
         key_quantize(0, 1)
         q_quantize(0)
-        key_scale(2, 1, 0)
-        x_copy(1, 1)
-        key_copy(1, 0, 0)
-        key_copy(1, 0, 1)
-        scores(0, 0)
-        scores(0, 1)
-        x_quantize(1)
-        key_scale(2, 1, 1)
-        negate_and_min(0, 0)
-        key_quantize(1, 0)
-        negate_and_min(0, 1)
-        q_matmul(1)
-        key_turn(1, 1, 0)
+        q_interleave(1, nc.scalar.copy)
         key_turn(1, 1, 1)
-        scores(1, 0)
-        scores(1, 1)
-        x_turn(2, 0)
-        q_bias(1)
-        key_copy(1, 1, 0)
-        key_copy(1, 1, 1)
-        exponentials(0)
-        x_copy(2, 0)
-        x_turn(2, 1)
-        key_turn(2, 0, 0)
-        key_turn(2, 0, 1)
-        q_interleave(1)
-        negate_and_min(1, 0)
-        q_quantize(1)
-        negate_and_min(1, 1)
-        key_quantize(1, 1)
-        invert(0)
-        finish(0)
-        x_copy(2, 1)
-        exponentials(1)
-        key_copy(2, 0, 0)
-        key_copy(2, 0, 1)
-        scores(2, 0)
-        scores(2, 1)
+        key_quantize(1, 0)
         x_quantize(2)
-        invert(1)
-        negate_and_min(2, 0)
-        finish(1)
-        negate_and_min(2, 1)
-        key_quantize(2, 0)
-        q_matmul(2)
+
+        for h in range(2):
+            for i in range(2):
+                scores(i, h)
+        row_extreme(0, 0)
+        row_extreme(1, 0)
+        row_extreme(0, 1)
+        exponentials(0)
+        mask_on_gpsimd(0, M)
+        q_project(2)
+        q_quantize(1)
+        key_quantize(1, 1)
+        scores(2, 0)
+        row_extreme(1, 1)
+        exponentials(1)
+        mask_on_gpsimd(1, M)
+        scores(2, 1)
+        q_interleave(2, nc.scalar.copy)
+        key_scale_and_turn(2, 0, 0)
+        invert(0)
+        row_extreme(2, 0)
         scores(3, 0)
-        key_turn(2, 1, 0)
-        key_turn(2, 1, 1)
-        scores(3, 1)
-        negate_and_min(3, 0)
-        q_bias(2)
-        key_copy(2, 1, 0)
-        key_copy(2, 1, 1)
+        key_scale(2, 0, 1)
+        row_extreme(2, 1)
         exponentials(2)
-        q_interleave(2)
-        negate_and_min(3, 1)
-        q_quantize(2)
-        invert(2)
-        key_quantize(2, 1)
-        finish(2)
+        mask_on_gpsimd(2, TILE2_ON_GPSIMD)
+        scores(3, 1)
+        key_turn(2, 0, 1)
+        for s in range(2):
+            key_scale_and_turn(2, 1, s)
+        for h in range(2):
+            invert(1 + h)
+            row_extreme(3, h)
         exponentials(3)
+
+        key_quantize(2, 0)
+        q_quantize(2)
         scores(4, 0)
         scores(5, 0)
-        negate_and_min(4, 0)
-        negate_and_min(5, 0)
+        key_quantize(2, 1)
         scores(4, 1)
         scores(5, 1)
-        negate_and_min(4, 1)
+        finish_on_vector(2, TILE2_ON_GPSIMD, M - TILE2_ON_GPSIMD)
+        for i, width in ((0, M), (1, M), (2, TILE2_ON_GPSIMD)):
+            normalise_on_scalar(i, width)
         invert(3)
-        negate_and_min(5, 1)
-        finish(3)
-        exponentials(4)
-        exponentials(5)
+        for h in range(2):
+            for i in (4, 5):
+                row_extreme(i, h)
+        for i in (4, 5):
+            exponentials(i)
+
+        finish_on_vector(3, 0, M)
         invert(4)
-        finish(4)
+        finish_on_vector(4, 0, M)
         invert(5)
-        finish(5, 2)
+        for h in range(2):
+            finish_on_vector(5, h * HALF, HALF)

@@ -19,7 +19,6 @@ P = 128
 PACK = 4
 K_PASS = P * PACK
 HALF = M // 2
-W_SPLIT = DQK // 2
 TURN_BANKS = 3
 SUM_BANKS = 4
 RING = 3
@@ -59,11 +58,11 @@ def tile_text2imgca_pa_kernel(tc, x1, Wq, bq, k_img_bytes, k_img_scale, masks, o
             nc.sync.dma_start(out=tile[:], in_=x1[b, a * P : (a + 1) * P, :])
             x_rows[b, a] = tile
 
-        def load_w(g, first, width):
-            tile = sb("w_rows_%d_%d" % (g, first), [P, PACK, width], BF16)
-            src = Wq[g * K_PASS : (g + 1) * K_PASS, first : first + width]
+        def load_w(g):
+            tile = sb("w_rows_%d" % g, [P, PACK, DQK], BF16)
+            src = Wq[g * K_PASS : (g + 1) * K_PASS, :]
             nc.sync.dma_start(out=tile[:], in_=src.rearrange("(p j) d -> p j d", j=PACK))
-            w_rows[g, first] = tile
+            w_rows[g] = tile
 
         def load_mask(b):
             tile = sb("mask_rows_%d" % b, [P, 2, M], BF16)
@@ -72,10 +71,9 @@ def tile_text2imgca_pa_kernel(tc, x1, Wq, bq, k_img_bytes, k_img_scale, masks, o
 
         scale_cols = sb("scale_cols", [P, PACK], F32)
         nc.sync.dma_start(out=scale_cols[:], in_=k_img_scale.rearrange("o i (p c) -> p (o i c)", c=PACK))
-        load_w(0, 0, W_SPLIT)
         load_keys(0, 0)
-        load_w(1, 0, DQK)
-        load_w(0, W_SPLIT, W_SPLIT)
+        load_w(0)
+        load_w(1)
         load_keys(0, 1)
         load_x(0, 0)
         load_x(0, 1)
@@ -125,13 +123,16 @@ def tile_text2imgca_pa_kernel(tc, x1, Wq, bq, k_img_bytes, k_img_scale, masks, o
             key_mx[b, h] = quantize("key_%d_%d" % (b, h), src, HALF)
 
         w_in, w_mx = {}, {}
-        for g in range(2):
-            w_in[g] = sb("w_in_%d" % g, [P, PACK, P, PACK], BF16)
 
-        def w_views(g, first):
-            src = w_rows[g, first][:].rearrange("p j (m t) -> p m t j", t=PACK)
-            dst = w_in[g][:].rearrange("p t m j -> p m t j")
-            return dst[:, first // PACK : first // PACK + src.shape[1]], src
+        def w_interleave(g, copy):
+            w_in[g] = sb("w_in_%d" % g, [P, PACK, P, PACK], BF16)
+            copy(
+                out=w_in[g][:].rearrange("p t m j -> p m t j"),
+                in_=w_rows[g][:].rearrange("p j (m t) -> p m t j", t=PACK),
+            )
+
+        def gpsimd_copy(out, in_):
+            nc.gpsimd.tensor_scalar(out=out, in0=in_, scalar1=1.0, scalar2=0.0, op0=ALU.mult, op1=ALU.add)
 
         def w_quantize(g):
             w_mx[g] = quantize("w_%d" % g, w_in[g][:].rearrange("p t m j -> p (t m j)"), DQK)
@@ -252,12 +253,8 @@ def tile_text2imgca_pa_kernel(tc, x1, Wq, bq, k_img_bytes, k_img_scale, masks, o
             )
             nc.sync.dma_start(out=out[b, a * P : (a + 1) * P, cols], in_=res[:])
 
-        dst, src = w_views(0, 0)
-        nc.vector.tensor_copy(out=dst, in_=src)
-        dst, src = w_views(1, 0)
-        nc.gpsimd.tensor_scalar(out=dst, in0=src, scalar1=1.0, scalar2=0.0, op0=ALU.mult, op1=ALU.add)
-        dst, src = w_views(0, W_SPLIT)
-        nc.scalar.copy(out=dst, in_=src)
+        w_interleave(0, nc.scalar.copy)
+        w_interleave(1, gpsimd_copy)
         for s in range(2):
             key_scale_and_turn(0, 0, s)
         for a in range(2):

from contextlib import ExitStack

import concourse.mybir as mybir
from concourse.masks import make_identity

B, N, M, TC, DQK = 3, 256, 1024, 1024, 512
FLOPS = 2 * B * N * TC * DQK + 2 * B * N * DQK * M

F32 = mybir.dt.float32
BF16 = mybir.dt.bfloat16
U32 = mybir.dt.uint32
U8 = mybir.dt.uint8
FP8 = mybir.dt.float8_e4m3fn
FP8X4 = mybir.dt.float8_e4m3fn_x4
ALU = mybir.AluOpType
ACT = mybir.ActivationFunctionType

P = 128
PACK = 4
K_PASS = P * PACK
HALF = M // 2
TURN_BANKS = 3
SUM_BANKS = 4
RING = 3
TILE2_ON_GPSIMD = M // 2


def tile_text2imgca_pa_kernel(tc, x1, Wq, bq, k_img_bytes, k_img_scale, masks, out):
    nc = tc.nc
    with ExitStack() as ctx:
        keep = ctx.enter_context(tc.tile_pool(name="keep", bufs=1))
        ring = ctx.enter_context(tc.tile_pool(name="ring", bufs=RING))
        psum = ctx.enter_context(tc.psum_pool(name="psum", bufs=1))
        ctx.enter_context(tc.manual_schedule())

        def sb(name, shape, dtype):
            return keep.tile(shape, dtype, name=name, align_bytes=64)

        def quantize(name, src, columns):
            codes = sb(name + "_codes", [P, columns], U32)
            scales = sb(name + "_scales", [P, columns], U8)
            nc.vector.quantize_mx(out=codes[:].bitcast(FP8X4), scales=scales[:], in_=src)
            return codes, scales

        ident = sb("ident", [P, P], F32)
        make_identity(nc, ident[:])

        key_bytes, x_rows, w_rows, mask_rows = {}, {}, {}, {}

        def load_keys(b, h):
            tile = sb("key_bytes_%d_%d" % (b, h), [P, PACK * DQK], U8)
            src = k_img_bytes[b, h * HALF : (h + 1) * HALF, :]
            nc.sync.dma_start(out=tile[:], in_=src.rearrange("(p r) d -> p (r d)", r=PACK))
            key_bytes[b, h] = tile

        def load_x(b, a):
            tile = sb("x_rows_%d_%d" % (b, a), [P, TC], BF16)
            nc.sync.dma_start(out=tile[:], in_=x1[b, a * P : (a + 1) * P, :])
            x_rows[b, a] = tile

        def load_w(g):
            tile = sb("w_rows_%d" % g, [P, PACK, DQK], BF16)
            src = Wq[g * K_PASS : (g + 1) * K_PASS, :]
            nc.sync.dma_start(out=tile[:], in_=src.rearrange("(p j) d -> p j d", j=PACK))
            w_rows[g] = tile

        def load_mask(b):
            tile = sb("mask_rows_%d" % b, [P, 2, M], BF16)
            nc.sync.dma_start(out=tile[:], in_=masks[b].rearrange("(a p) m -> p a m", p=P))
            mask_rows[b] = tile

        scale_cols = sb("scale_cols", [P, PACK], F32)
        nc.sync.dma_start(out=scale_cols[:], in_=k_img_scale.rearrange("o i (p c) -> p (o i c)", c=PACK))
        load_keys(0, 0)
        load_w(0)
        load_w(1)
        load_keys(0, 1)
        load_x(0, 0)
        load_x(0, 1)
        bias = sb("bias", [P, PACK], BF16)
        nc.sync.dma_start(out=bias[:], in_=bq.rearrange("(p t) -> p t", t=PACK))
        load_keys(1, 0)
        load_x(1, 0)
        load_x(1, 1)
        load_keys(1, 1)
        load_x(2, 0)
        load_x(2, 1)
        load_keys(2, 0)
        load_keys(2, 1)
        for b in range(B):
            load_mask(b)

        scale_bank = psum.tile([P, DQK], F32, name="scale_bank")
        for c in range(PACK):
            nc.tensor.transpose(scale_bank[:, c::PACK], scale_cols[:, c : c + 1].to_broadcast([P, P]), ident[:])

        key_wide, key_in, key_mx = {}, {}, {}

        def key_scale(b, h, s):
            tile = sb("key_wide_%d_%d_%d" % (b, h, s), [P, 2, DQK], BF16)
            for r in range(2):
                row = 2 * s + r
                codes = key_bytes[b, h][:, row * DQK : (row + 1) * DQK].bitcast(FP8)
                nc.vector.tensor_tensor(out=tile[:, r, :], in0=codes, in1=scale_bank[:], op=ALU.mult)
            key_wide[b, h, s] = tile

        def key_turn(b, h, s):
            bank = psum.tile([P, 4, P], F32, name="key_bank", tag="turn", bufs=TURN_BANKS)
            for r in range(2):
                pairs = key_wide[b, h, s][:, r, :].bitcast(F32)
                for u in range(2):
                    nc.tensor.transpose(bank[:, 2 * r + u, :], pairs[:, u::2], ident[:])
            if s == 0:
                key_in[b, h] = sb("key_in_%d_%d" % (b, h), [P, P, 2, 4], F32)
            nc.scalar.copy(out=key_in[b, h][:, :, s, :], in_=bank[:].rearrange("p j n -> p n j"))

        def key_scale_and_turn(b, h, s):
            key_scale(b, h, s)
            key_turn(b, h, s)

        def key_quantize(b, h):
            src = key_in[b, h][:].rearrange("p n s j -> p (n s j)").bitcast(BF16)
            key_mx[b, h] = quantize("key_%d_%d" % (b, h), src, HALF)

        w_in, w_mx = {}, {}

        def w_interleave(g, copy):
            w_in[g] = sb("w_in_%d" % g, [P, PACK, P, PACK], BF16)
            copy(
                out=w_in[g][:].rearrange("p t m j -> p m t j"),
                in_=w_rows[g][:].rearrange("p j (m t) -> p m t j", t=PACK),
            )

        def gpsimd_copy(out, in_):
            nc.gpsimd.tensor_scalar(out=out, in0=in_, scalar1=1.0, scalar2=0.0, op0=ALU.mult, op1=ALU.add)

        def w_quantize(g):
            w_mx[g] = quantize("w_%d" % g, w_in[g][:].rearrange("p t m j -> p (t m j)"), DQK)

        x_in, x_mx = {}, {}

        def x_turn(b, a):
            bank = psum.tile([P, 4, P], F32, name="x_bank", tag="turn", bufs=TURN_BANKS)
            pairs = x_rows[b, a][:].bitcast(F32)
            for g in range(2):
                for u in range(2):
                    first = g * K_PASS // 2
                    nc.tensor.transpose(bank[:, 2 * g + u, :], pairs[:, first + u : first + K_PASS // 2 : 2], ident[:])
            if a == 0:
                x_in[b] = sb("x_in_%d" % b, [P, 2, N, 2], F32)
            nc.scalar.copy(
                out=x_in[b][:, :, a * P : (a + 1) * P, :],
                in_=bank[:].rearrange("p (g u) n -> p g n u", u=2),
            )

        def x_quantize(b):
            x_mx[b] = quantize("x_%d" % b, x_in[b][:].rearrange("p g n u -> p (g n u)").bitcast(BF16), 2 * N)

        q_slices, q_in, q_mx = {}, {}, {}

        def q_project(b):
            x_codes, x_scales = x_mx[b]
            banks = []
            for pair in range(2):
                bank = psum.tile([P, 2, N], F32, name="q_bank", tag="sums", bufs=SUM_BANKS)
                for e in range(2):
                    cols = slice((2 * pair + e) * P, (2 * pair + e + 1) * P)
                    for g in range(2):
                        w_codes, w_scales = w_mx[g]
                        nc.tensor.matmul_mx(
                            out=bank[:, e, :],
                            lhsT=w_codes[:, cols].bitcast(FP8X4),
                            lhsT_scale=w_scales[:, cols],
                            rhs=x_codes[:, g * N : (g + 1) * N].bitcast(FP8X4),
                            rhs_scale=x_scales[:, g * N : (g + 1) * N],
                            start=(g == 0),
                            stop=(g == 1),
                        )
                banks.append(bank)
            q_slices[b] = sb("q_slices_%d" % b, [P, PACK, N], BF16)
            for t in range(PACK):
                nc.scalar.activation(
                    out=q_slices[b][:, t, :], in_=banks[t // 2][:, t % 2, :], func=ACT.Identity, bias=bias[:, t : t + 1]
                )

        def q_interleave(b, copy):
            q_in[b] = sb("q_in_%d" % b, [P, N, PACK], BF16)
            copy(out=q_in[b][:], in_=q_slices[b][:].rearrange("p t n -> p n t"))

        def q_quantize(b):
            q_mx[b] = quantize("q_%d" % b, q_in[b][:].rearrange("p n t -> p (n t)"), N)

        score_bank, negated, low, expd, total, inv, masked = {}, {}, {}, {}, {}, {}, {}

        def scores(i, h):
            b, a = divmod(i, 2)
            q_codes, q_scales = q_mx[b]
            k_codes, k_scales = key_mx[b, h]
            bank = psum.tile([P, HALF], F32, name="score_bank", tag="sums", bufs=SUM_BANKS)
            nc.tensor.matmul_mx(
                out=bank[:],
                lhsT=q_codes[:, a * P : (a + 1) * P].bitcast(FP8X4),
                lhsT_scale=q_scales[:, a * P : (a + 1) * P],
                rhs=k_codes[:].bitcast(FP8X4),
                rhs_scale=k_scales[:],
                start=True,
                stop=True,
            )
            score_bank[i, h] = bank

        def row_extreme(i, h):
            if h == 0:
                negated[i] = ring.tile([P, M], F32, name="negated")
            low[i, h] = sb("low_%d_%d" % (i, h), [P, 1], F32)
            nc.vector.tensor_scalar(
                out=negated[i][:, h * HALF : (h + 1) * HALF],
                in0=score_bank[i, h][:],
                scalar1=-1.0,
                scalar2=low[i, 0][:] if h else None,
                op0=ALU.mult,
                op1=ALU.min,
                accum_out=low[i, h][:],
            )

        def exponentials(i):
            expd[i] = ring.tile([P, M], F32, name="expd")
            total[i] = sb("total_%d" % i, [P, 1], F32)
            nc.scalar.activation(
                out=expd[i][:], in_=negated[i][:], func=ACT.Exp, scale=-1.0, bias=low[i, 1][:], accum_out=total[i][:]
            )

        def invert(i):
            inv[i] = sb("inv_%d" % i, [P, 1], F32)
            nc.vector.reciprocal(out=inv[i][:], in_=total[i][:])

        def mask_on_gpsimd(i, width):
            b, a = divmod(i, 2)
            masked[i] = ring.tile([P, width], F32, name="masked")
            nc.gpsimd.tensor_tensor(out=masked[i][:], in0=expd[i][:, :width], in1=mask_rows[b][:, a, :width], op=ALU.mult)

        def normalise_on_scalar(i, width):
            b, a = divmod(i, 2)
            res = sb("res_scalar_%d" % i, [P, width], F32)
            nc.scalar.activation(out=res[:], in_=masked[i][:], func=ACT.Copy, scale=inv[i][:])
            nc.sync.dma_start(out=out[b, a * P : (a + 1) * P, :width], in_=res[:])

        def finish_on_vector(i, first, width):
            b, a = divmod(i, 2)
            cols = slice(first, first + width)
            res = sb("res_vector_%d_%d" % (i, first), [P, width], F32)
            nc.vector.scalar_tensor_tensor(
                out=res[:], in0=expd[i][:, cols], scalar=inv[i][:], in1=mask_rows[b][:, a, cols], op0=ALU.mult, op1=ALU.mult
            )
            nc.sync.dma_start(out=out[b, a * P : (a + 1) * P, cols], in_=res[:])

        w_interleave(0, nc.scalar.copy)
        w_interleave(1, gpsimd_copy)
        for s in range(2):
            key_scale_and_turn(0, 0, s)
        for a in range(2):
            x_turn(0, a)
        for s in range(2):
            x_turn(1, s)
            key_scale_and_turn(0, 1, s)
        key_scale_and_turn(1, 0, 0)

        for g in range(2):
            w_quantize(g)
        x_quantize(0)
        q_project(0)
        key_scale_and_turn(1, 0, 1)
        key_quantize(0, 0)
        for a in range(2):
            x_turn(2, a)
        key_scale(1, 1, 0)
        x_quantize(1)
        q_project(1)
        key_turn(1, 1, 0)
        key_scale(1, 1, 1)
        q_interleave(0, nc.vector.tensor_copy)
        key_quantize(0, 1)
        q_quantize(0)
        q_interleave(1, nc.scalar.copy)
        key_turn(1, 1, 1)
        key_quantize(1, 0)
        x_quantize(2)

        for h in range(2):
            for i in range(2):
                scores(i, h)
        row_extreme(0, 0)
        row_extreme(1, 0)
        row_extreme(0, 1)
        exponentials(0)
        mask_on_gpsimd(0, M)
        q_project(2)
        q_quantize(1)
        key_quantize(1, 1)
        scores(2, 0)
        row_extreme(1, 1)
        exponentials(1)
        mask_on_gpsimd(1, M)
        scores(2, 1)
        q_interleave(2, nc.scalar.copy)
        key_scale_and_turn(2, 0, 0)
        invert(0)
        row_extreme(2, 0)
        scores(3, 0)
        key_scale(2, 0, 1)
        row_extreme(2, 1)
        exponentials(2)
        mask_on_gpsimd(2, TILE2_ON_GPSIMD)
        scores(3, 1)
        key_turn(2, 0, 1)
        for s in range(2):
            key_scale_and_turn(2, 1, s)
        for h in range(2):
            invert(1 + h)
            row_extreme(3, h)
        exponentials(3)

        key_quantize(2, 0)
        q_quantize(2)
        scores(4, 0)
        scores(5, 0)
        key_quantize(2, 1)
        scores(4, 1)
        scores(5, 1)
        finish_on_vector(2, TILE2_ON_GPSIMD, M - TILE2_ON_GPSIMD)
        for i, width in ((0, M), (1, M), (2, TILE2_ON_GPSIMD)):
            normalise_on_scalar(i, width)
        invert(3)
        for h in range(2):
            for i in (4, 5):
                row_extreme(i, h)
        for i in (4, 5):
            exponentials(i)

        finish_on_vector(3, 0, M)
        invert(4)
        finish_on_vector(4, 0, M)
        invert(5)
        for h in range(2):
            finish_on_vector(5, h * HALF, HALF)
